import numpy as np
import ml_dtypes


def mxq(x, axis, fmt="e4m3"):
    dtype, down = {"e4m3": (ml_dtypes.float8_e4m3fn, 7), "e5m2": (ml_dtypes.float8_e5m2, 14)}[fmt]
    v = np.moveaxis(np.asarray(x, np.float32).astype(ml_dtypes.bfloat16).astype(np.float64), axis, -1)
    blocks = v.reshape(v.shape[:-1] + (-1, 32))
    amax = np.abs(blocks).max(-1, keepdims=True)
    byte = np.maximum(np.where(amax > 0, np.frexp(amax)[1] - 1 + 127, 0) - down, 1)
    scale = np.exp2(byte - 127.0)
    codes = (blocks / scale).astype(np.float32).astype(dtype).astype(np.float64)
    return np.moveaxis((codes * scale).reshape(v.shape), -1, axis)


WIDE = False


def mx_kscale(k):
    if not WIDE:
        return np.ones(k)
    levels = np.array([10, -10, 5, -5, 0])
    a = np.random.permutation(np.resize(levels, k // 512 * 4)).reshape(k // 512, 4)
    idx = np.arange(k)
    return np.exp2(a[idx // 512, idx % 128 // 32])


BF16 = ml_dtypes.bfloat16


def bf(x):
    return np.asarray(x, np.float32).astype(BF16)


def f64(x):
    return np.asarray(x).astype(np.float64)


B, N, D, F, O = 32, 32, 512, 512, 512
NEG = -1e9


def erf(v):
    a = np.clip(v, -6.0, 6.0)
    a2 = 2.0 * a * a
    top = a2.max()
    term, tot, r, n = a.copy(), a.copy(), 1.0, 0
    while r > 1e-18:
        n += 1
        r *= top / (2 * n + 1)
        term *= a2
        term /= 2 * n + 1
        tot += term
    return 2.0 / np.sqrt(np.pi) * np.exp(-a * a) * tot


def gelu(v):
    return 0.5 * v * (1.0 + erf(v / np.sqrt(2.0)))


def setup_inputs():
    s = mx_kscale(D)
    return {"x": bf(np.random.standard_normal((B, N, D)) * s),
            "W1": bf(np.random.standard_normal((2 * D, F)) / np.sqrt(2 * D) / np.tile(s, 2)[:, None]),
            "b1": bf(np.random.standard_normal(F) * 0.2),
            "W2": bf(np.random.standard_normal((F, O)) / np.sqrt(F)),
            "b2": bf(np.random.standard_normal(O) * 0.2)}


def reference(x, W1, b1, W2, b2):
    xq = mxq(f64(x), 2, "e4m3")
    W1 = f64(W1)
    ai = xq @ mxq(W1[:D], 0, "e4m3")
    aj = xq @ mxq(W1[D:], 0, "e4m3")
    ii, jj = np.tril_indices(N)
    h = gelu(ai[:, ii, :] + aj[:, jj, :] + f64(b1))
    pu = (mxq(h, 2, "e4m3") @ mxq(f64(W2), 0, "e4m3")) + f64(b2)
    p = np.zeros((B, N, N, O))
    p[:, ii, jj, :] = pu
    mask = np.triu(np.ones((N, N), dtype=bool), 1)
    sq = np.sum(p * p, axis=-1)
    s = np.sqrt(np.where(mask[None], 1.0, sq))
    s = np.where(mask[None], NEG, s)
    e = np.exp(s - s.max(-1, keepdims=True))
    w = e / e.sum(-1, keepdims=True)
    return np.sum(w[..., None] * p, axis=2)

@@ -1,0 +1,281 @@
+from contextlib import ExitStack
+
+import concourse.mybir as mybir
+from concourse.masks import make_identity
+
+FLOPS = 2 * 1024 * 1024 * 512 + 2 * 16896 * 512 * 512
+
+F32 = mybir.dt.float32
+BF16 = mybir.dt.bfloat16
+U32 = mybir.dt.uint32
+U8 = mybir.dt.uint8
+FP8X4 = mybir.dt.float8_e4m3fn_x4
+ALU = mybir.AluOpType
+ACT = mybir.ActivationFunctionType
+AX = mybir.AxisListType
+
+P = 128
+PADL = 128
+NCOL = PADL + 1024 + 32
+NEG = -1.0e9
+NC_RING = 44
+N_PE = (1, 2, 3, 4, 6, 7, 8, 9)
+REGROUP = "G"
+
+
+def tile_pairconnect_kernel(tc, x, W1, b1, W2, b2, out):
+    nc = tc.nc
+    with ExitStack() as ctx:
+        const = ctx.enter_context(tc.tile_pool(name="const", bufs=1))
+        pro = ctx.enter_context(tc.tile_pool(name="pro", bufs=1))
+        work = ctx.enter_context(tc.tile_pool(name="work", bufs=3))
+        cpool = ctx.enter_context(tc.tile_pool(name="cring", bufs=NC_RING))
+        small = ctx.enter_context(tc.tile_pool(name="small", bufs=3))
+        zpool = ctx.enter_context(tc.psum_pool(name="zps", bufs=1))
+        ppool = ctx.enter_context(tc.psum_pool(name="pps", bufs=3))
+        apool = ctx.enter_context(tc.psum_pool(name="aps", bufs=1))
+        dpool = ctx.enter_context(tc.tile_pool(name="diag", bufs=4))
+
+        xr = pro.tile([P, 4096], BF16)
+        xv = x.flatten_outer_dims().rearrange("(n p) k -> p n k", p=P)
+        xrv = xr[:].rearrange("p (n k) -> p n k", n=8)
+        nc.sync.dma_start(out=xrv[:, 0:4, :], in_=xv[:, 0:4, :])
+        nc.sync.dma_start(out=xrv[:, 4:8, :], in_=xv[:, 4:8, :])
+        w1r = pro.tile([P, 4096], BF16)
+        nc.sync.dma_start(
+            out=w1r[:].rearrange("p (a f) -> p a f", a=4),
+            in_=W1.rearrange("(a q e) c -> q a (e c)", a=4, q=P, e=2),
+        )
+        w2r = pro.tile([P, 2048], BF16)
+        nc.sync.dma_start(
+            out=w2r[:].rearrange("p (t n) -> p t n", t=4),
+            in_=W2.rearrange("(p t) n -> p t n", t=4),
+        )
+        b1r = pro.tile([P, 4], BF16)
+        nc.sync.dma_start(out=b1r[:], in_=b1.rearrange("(p t) -> p t", t=4))
+        b2r = pro.tile([P, 512], BF16)
+        nc.sync.dma_start(out=b2r[:], in_=b2.partition_broadcast(P))
+
+        ident = const.tile([P, P], F32)
+        make_identity(nc, ident[:])
+
+        xg = pro.tile([P, NCOL * 4], BF16, align_bytes=64)
+        xg32 = xg[:].bitcast(F32)
+        nc.vector.memset(xg32[:, 0 : 2 * PADL], 0.0)
+        nc.vector.memset(xg32[:, 2 * (PADL + 1024) : 2 * NCOL], 0.0)
+        xr32 = xr[:].bitcast(F32)
+        xbody = xg32[:, 2 * PADL : 2 * PADL + 2048].rearrange(
+            "p (i b u) -> p i b u", i=32, b=32, u=2
+        )
+        for j in range(4):
+            pt = ppool.tile([P, 512], F32, tag="pp")
+            for u in range(2):
+                for n2 in range(2):
+                    off = u * 256 + n2 * 128
+                    src0 = (2 * j + n2) * 256 + u * 128
+                    nc.tensor.transpose(pt[:, off : off + 128], xr32[:, src0 : src0 + 128], ident[:])
+            src = pt[:].rearrange("p (u c i) -> p i c u", u=2, c=8, i=32)
+            dst = xbody[:, :, 8 * j : 8 * j + 8, :]
+            if j % 2 == 0:
+                nc.vector.tensor_copy(out=dst, in_=src)
+            else:
+                nc.scalar.copy(out=dst, in_=src)
+
+        ca = const.tile([P, 1152], U32, align_bytes=64)
+        sa = const.tile([P, 1152], U8, align_bytes=64)
+        cb = const.tile([P, 1152], U32, align_bytes=64)
+        sb = const.tile([P, 1152], U8, align_bytes=64)
+
+        w1g = pro.tile([P, 4096], BF16, align_bytes=64)
+        w1c = const.tile([P, 1024], U32, align_bytes=64)
+        w1s = const.tile([P, 1024], U8, align_bytes=64)
+        for h in range(2):
+            nc.vector.tensor_copy(
+                out=w1g[:, h * 2048 : (h + 1) * 2048].rearrange("p (q m t) -> p q m t", q=4, m=P, t=4),
+                in_=w1r[:, h * 2048 : (h + 1) * 2048].rearrange("p (t m q) -> p q m t", t=4, m=P, q=4),
+            )
+        nc.vector.quantize_mx(out=ca[:, 0:1024].bitcast(FP8X4), scales=sa[:, 0:1024], in_=xg[:, 0:4096])
+        nc.vector.quantize_mx(out=ca[:, 1024:1152].bitcast(FP8X4), scales=sa[:, 1024:1152], in_=xg[:, 4096:4608])
+        for h in range(2):
+            nc.vector.quantize_mx(
+                out=w1c[:, h * 512 : (h + 1) * 512].bitcast(FP8X4),
+                scales=w1s[:, h * 512 : (h + 1) * 512],
+                in_=w1g[:, h * 2048 : (h + 1) * 2048],
+            )
+        nc.vector.quantize_mx(out=cb[:, 0:1024].bitcast(FP8X4), scales=sb[:, 0:1024], in_=xg[:, 128:4224])
+        nc.vector.quantize_mx(out=cb[:, 1024:1152].bitcast(FP8X4), scales=sb[:, 1024:1152], in_=xg[:, 4224:4736])
+
+        w2g = pro.tile([P, 2048], BF16, align_bytes=64)
+        w2c = const.tile([P, 512], U32, align_bytes=64)
+        w2s = const.tile([P, 512], U8, align_bytes=64)
+        nc.vector.tensor_copy(
+            out=w2g[:].rearrange("p (n t) -> p n t", t=4),
+            in_=w2r[:].rearrange("p (t n) -> p n t", t=4),
+        )
+        b1f = const.tile([P, 4], F32)
+        nc.vector.tensor_copy(out=b1f[:], in_=b1r[:])
+        nc.vector.quantize_mx(out=w2c[:].bitcast(FP8X4), scales=w2s[:], in_=w2g[:])
+        b2b = const.tile([P, 512], F32)
+        nc.vector.tensor_copy(out=b2b[:], in_=b2r[:])
+        negm = const.tile([P, 8 * 32], F32)
+        nc.gpsimd.memset(negm[:], 0.0)
+        for m in range(8):
+            for d0 in range(1, 4):
+                c = 32 * m + d0 * (m + 1)
+                nc.gpsimd.memset(negm[0 : 32 * d0, c : c + 1], NEG)
+        half = const.tile([P, 4], F32)
+        nc.gpsimd.memset(half[:], 0.5)
+
+        pending = []
+        head = [0]
+        nquad = [0]
+
+        def emit_wacc(count):
+            for unused in range(min(count, len(pending) - head[0])):
+                ct, wcol, st, on_pe = pending[head[0]]
+                head[0] += 1
+                if on_pe:
+                    if st["npe"] == 0:
+                        st["ab"] = apool.tile([P, 512], F32, name="ab_acc", tag="ab")
+                    dg = dpool.tile([P, P], F32, tag="dg")
+                    nc.gpsimd.tensor_scalar(out=dg[:], in0=ident[:], scalar1=wcol, scalar2=0.0, op0=ALU.mult, op1=ALU.add)
+                    st["npe"] += 1
+                    nc.tensor.matmul(
+                        out=st["ab"][:], lhsT=dg[:], rhs=ct[:], start=(st["npe"] == 1), stop=(st["npe"] == st["pe_total"])
+                    )
+                elif st["nv"] == 0:
+                    st["o"] = work.tile([P, 512], F32, name="o_acc", tag="o")
+                    nc.vector.tensor_scalar(out=st["o"][:], in0=ct[:], scalar1=wcol, scalar2=None, op0=ALU.mult)
+                    st["nv"] += 1
+                else:
+                    nc.vector.scalar_tensor_tensor(
+                        out=st["o"][:], in0=ct[:], scalar=wcol, in1=st["o"][:], op0=ALU.mult, op1=ALU.add
+                    )
+                    st["nv"] += 1
+                if st["nv"] + st["npe"] == st["total"]:
+                    if st["pe_total"] > 0:
+                        nc.vector.tensor_tensor(out=st["o"][:], in0=st["ab"][:], in1=st["o"][:], op=ALU.add)
+                    for r in range(4):
+                        nc.sync.dma_start(out=out[:, 4 * st["m"] + r, :], in_=st["o"][32 * r : 32 * r + 32, :])
+
+        for m in range(7, -1, -1):
+            nd = 4 * (m + 1)
+            tiles = [(d0, kap) for d0 in range(4) for kap in range(m + 1)]
+            ssq = small.tile([P, 32], F32, tag="ssq")
+            sc = small.tile([P, 32], F32, tag="sc")
+            cts = []
+            per_quad = -(-(len(pending) - head[0]) // (m + 1))
+            for g in range(m + 1):
+                quad = tiles[4 * g : 4 * g + 4]
+                hp = work.tile([P, 2048], BF16, tag="hp")
+                for tq in range(4):
+                    zt = zpool.tile([P, 512], F32, name="zt", tag="z%d" % tq)
+                    for pos in range(4):
+                        d0, kap = quad[pos]
+                        cs = PADL + 128 * kap - 32 * d0
+                        if d0 % 2 == 0:
+                            xjc, xjs = ca, sa
+                        else:
+                            xjc, xjs = cb, sb
+                            cs -= 32
+                        ci = PADL + 128 * m
+                        zo = zt[:, 128 * pos : 128 * pos + 128]
+                        nc.tensor.matmul_mx(
+                            out=zo,
+                            lhsT=w1c[:, tq * 128 : tq * 128 + 128].bitcast(FP8X4),
+                            lhsT_scale=w1s[:, tq * 128 : tq * 128 + 128],
+                            rhs=ca[:, ci : ci + 128].bitcast(FP8X4),
+                            rhs_scale=sa[:, ci : ci + 128],
+                            start=True,
+                            stop=False,
+                        )
+                        nc.tensor.matmul_mx(
+                            out=zo,
+                            lhsT=w1c[:, 512 + tq * 128 : 512 + tq * 128 + 128].bitcast(FP8X4),
+                            lhsT_scale=w1s[:, 512 + tq * 128 : 512 + tq * 128 + 128],
+                            rhs=xjc[:, cs : cs + 128].bitcast(FP8X4),
+                            rhs_scale=xjs[:, cs : cs + 128],
+                            start=False,
+                            stop=True,
+                        )
+                    nc.scalar.activation(
+                        out=hp[:, tq * 512 : (tq + 1) * 512],
+                        in_=zt[:],
+                        func=ACT.Gelu,
+                        bias=b1f[:, tq : tq + 1],
+                        scale=1.0,
+                    )
+                hg = work.tile([P, 2048], BF16, tag="hg", align_bytes=64)
+                eng = REGROUP[nquad[0] % len(REGROUP)]
+                nquad[0] += 1
+                if eng == "V":
+                    nc.vector.tensor_copy(
+                        out=hg[:].rearrange("p (c i t) -> p c t i", i=4, t=4),
+                        in_=hp[:].rearrange("p (t c i) -> p c t i", t=4, i=4),
+                    )
+                elif eng == "S":
+                    nc.scalar.copy(
+                        out=hg[:].rearrange("p (c i t) -> p c t i", i=4, t=4),
+                        in_=hp[:].rearrange("p (t c i) -> p c t i", t=4, i=4),
+                    )
+                else:
+                    nc.gpsimd.tensor_scalar(
+                        out=hg[:].rearrange("p (c t) -> p c t", t=4),
+                        in0=hp[:].rearrange("p (t c) -> p c t", t=4),
+                        scalar1=1.0,
+                        scalar2=0.0,
+                        op0=ALU.mult,
+                        op1=ALU.add,
+                    )
+                hc = work.tile([P, 512], U32, tag="hc", align_bytes=64)
+                hs = work.tile([P, 512], U8, tag="hs", align_bytes=64)
+                nc.vector.quantize_mx(out=hc[:].bitcast(FP8X4), scales=hs[:], in_=hg[:])
+                for pos in range(4):
+                    d0, kap = quad[pos]
+                    col = 4 * g + pos
+                    pp = ppool.tile([P, 512], F32, tag="pp")
+                    nc.tensor.matmul_mx(
+                        out=pp[:],
+                        lhsT=hc[:, 128 * pos : 128 * pos + 128].bitcast(FP8X4),
+                        lhsT_scale=hs[:, 128 * pos : 128 * pos + 128],
+                        rhs=w2c[:].bitcast(FP8X4),
+                        rhs_scale=w2s[:],
+                        start=True,
+                        stop=True,
+                    )
+                    ct = cpool.tile([P, 512], F32, tag="c")
+                    nc.vector.tensor_tensor(out=ct[:], in0=pp[:], in1=b2b[:], op=ALU.add)
+                    junk = work.tile([P, 512], BF16, tag="junk")
+                    nc.scalar.activation(out=junk[:], in_=ct[:], func=ACT.Square, accum_out=ssq[:, col : col + 1])
+                    cts.append((ct, col))
+                nc.gpsimd.tensor_tensor(out=sc[:, 4 * g : 4 * g + 4], in0=ssq[:, 4 * g : 4 * g + 4], in1=half[:], op=ALU.pow)
+                emit_wacc(per_quad)
+            emit_wacc(len(pending))
+            sk = small.tile([P, 32], F32, tag="sk")
+            nc.vector.tensor_tensor(out=sk[:, 0:nd], in0=sc[:, 0:nd], in1=negm[:, 32 * m : 32 * m + nd], op=ALU.add)
+            mx = small.tile([P, 1], F32, tag="mx")
+            nc.vector.tensor_reduce(out=mx[:], in_=sk[:, 0:nd], axis=AX.X, op=ALU.max)
+            nh = small.tile([P, 1], F32, tag="nh")
+            nc.vector.tensor_scalar(out=nh[:], in0=mx[:], scalar1=-0.5, scalar2=None, op0=ALU.mult)
+            th = small.tile([P, 32], F32, tag="th")
+            nc.scalar.activation(out=th[:, 0:nd], in_=sk[:, 0:nd], func=ACT.Tanh, bias=nh[:, 0:1], scale=0.5)
+            bq = small.tile([P, 32], F32, tag="bq")
+            nc.vector.tensor_scalar(out=bq[:, 0:nd], in0=th[:, 0:nd], scalar1=-1.0, scalar2=1.0, op0=ALU.mult, op1=ALU.add)
+            rb = small.tile([P, 32], F32, tag="rb")
+            nc.vector.reciprocal(out=rb[:, 0:nd], in_=bq[:, 0:nd])
+            ex = small.tile([P, 32], F32, tag="ex")
+            se = small.tile([P, 1], F32, tag="se")
+            nc.vector.scalar_tensor_tensor(
+                out=ex[:, 0:nd], in0=th[:, 0:nd], scalar=1.0, in1=rb[:, 0:nd], op0=ALU.add, op1=ALU.mult, accum_out=se[:]
+            )
+            rs = small.tile([P, 1], F32, tag="rs")
+            nc.vector.reciprocal(out=rs[:], in_=se[:])
+            wt = small.tile([P, 32], F32, tag="wt")
+            nc.vector.tensor_scalar(out=wt[:, 0:nd], in0=ex[:, 0:nd], scalar1=rs[:, 0:1], scalar2=None, op0=ALU.mult)
+            npe = N_PE[m]
+            st = {"nv": 0, "npe": 0, "total": nd, "pe_total": npe, "m": m, "o": None, "ab": None}
+            for idx in range(nd):
+                ct, col = cts[idx]
+                on_pe = ((idx + 1) * npe) // nd > (idx * npe) // nd and idx > 0
+                pending.append((ct, wt[:, col : col + 1], st, on_pe))
+        emit_wacc(len(pending))

@@ -19,8 +19,8 @@ PADL = 128
 NCOL = PADL + 1024 + 32
 NEG = -1.0e9
 NC_RING = 44
-N_PE = (1, 2, 3, 4, 6, 7, 8, 9)
-REGROUP = "G"
+N_PE = (2, 3, 5, 6, 8, 10, 11, 13)
+REGROUP = "V"
 
 
 def tile_pairconnect_kernel(tc, x, W1, b1, W2, b2, out):

@@ -18,9 +18,16 @@ P = 128
 PADL = 128
 NCOL = PADL + 1024 + 32
 NEG = -1.0e9
-NC_RING = 44
+NC_RING = 52
 N_PE = (2, 3, 5, 6, 8, 10, 11, 13)
-REGROUP = "V"
+BLOCKS = (7, 6, 5, 4, 3, 2, 1, 0)
+NV = 3
+NP = 2
+MANUAL = True
+
+
+def regroup_on_scalar(k):
+    return False
 
 
 def tile_pairconnect_kernel(tc, x, W1, b1, W2, b2, out):
@@ -31,10 +38,10 @@ def tile_pairconnect_kernel(tc, x, W1, b1, W2, b2, out):
         work = ctx.enter_context(tc.tile_pool(name="work", bufs=3))
         cpool = ctx.enter_context(tc.tile_pool(name="cring", bufs=NC_RING))
         small = ctx.enter_context(tc.tile_pool(name="small", bufs=3))
+        dpool = ctx.enter_context(tc.tile_pool(name="diag", bufs=4))
         zpool = ctx.enter_context(tc.psum_pool(name="zps", bufs=1))
         ppool = ctx.enter_context(tc.psum_pool(name="pps", bufs=3))
         apool = ctx.enter_context(tc.psum_pool(name="aps", bufs=1))
-        dpool = ctx.enter_context(tc.tile_pool(name="diag", bufs=4))
 
         xr = pro.tile([P, 4096], BF16)
         xv = x.flatten_outer_dims().rearrange("(n p) k -> p n k", p=P)
@@ -90,10 +97,12 @@ def tile_pairconnect_kernel(tc, x, W1, b1, W2, b2, out):
         w1c = const.tile([P, 1024], U32, align_bytes=64)
         w1s = const.tile([P, 1024], U8, align_bytes=64)
         for h in range(2):
-            nc.vector.tensor_copy(
-                out=w1g[:, h * 2048 : (h + 1) * 2048].rearrange("p (q m t) -> p q m t", q=4, m=P, t=4),
-                in_=w1r[:, h * 2048 : (h + 1) * 2048].rearrange("p (t m q) -> p q m t", t=4, m=P, q=4),
-            )
+            dst = w1g[:, h * 2048 : (h + 1) * 2048].rearrange("p (q m t) -> p q m t", q=4, m=P, t=4)
+            src = w1r[:, h * 2048 : (h + 1) * 2048].rearrange("p (t m q) -> p q m t", t=4, m=P, q=4)
+            if h == 0:
+                nc.vector.tensor_copy(out=dst, in_=src)
+            else:
+                nc.scalar.copy(out=dst, in_=src)
         nc.vector.quantize_mx(out=ca[:, 0:1024].bitcast(FP8X4), scales=sa[:, 0:1024], in_=xg[:, 0:4096])
         nc.vector.quantize_mx(out=ca[:, 1024:1152].bitcast(FP8X4), scales=sa[:, 1024:1152], in_=xg[:, 4096:4608])
         for h in range(2):
@@ -102,21 +111,21 @@ def tile_pairconnect_kernel(tc, x, W1, b1, W2, b2, out):
                 scales=w1s[:, h * 512 : (h + 1) * 512],
                 in_=w1g[:, h * 2048 : (h + 1) * 2048],
             )
+        b1f = const.tile([P, 4], F32)
+        nc.vector.tensor_copy(out=b1f[:], in_=b1r[:])
         nc.vector.quantize_mx(out=cb[:, 0:1024].bitcast(FP8X4), scales=sb[:, 0:1024], in_=xg[:, 128:4224])
         nc.vector.quantize_mx(out=cb[:, 1024:1152].bitcast(FP8X4), scales=sb[:, 1024:1152], in_=xg[:, 4224:4736])
 
         w2g = pro.tile([P, 2048], BF16, align_bytes=64)
         w2c = const.tile([P, 512], U32, align_bytes=64)
         w2s = const.tile([P, 512], U8, align_bytes=64)
-        nc.vector.tensor_copy(
+        nc.scalar.copy(
             out=w2g[:].rearrange("p (n t) -> p n t", t=4),
             in_=w2r[:].rearrange("p (t n) -> p n t", t=4),
         )
-        b1f = const.tile([P, 4], F32)
-        nc.vector.tensor_copy(out=b1f[:], in_=b1r[:])
         nc.vector.quantize_mx(out=w2c[:].bitcast(FP8X4), scales=w2s[:], in_=w2g[:])
         b2b = const.tile([P, 512], F32)
-        nc.vector.tensor_copy(out=b2b[:], in_=b2r[:])
+        nc.gpsimd.tensor_copy(out=b2b[:], in_=b2r[:])
         negm = const.tile([P, 8 * 32], F32)
         nc.gpsimd.memset(negm[:], 0.0)
         for m in range(8):
@@ -126,156 +135,275 @@ def tile_pairconnect_kernel(tc, x, W1, b1, W2, b2, out):
         half = const.tile([P, 4], F32)
         nc.gpsimd.memset(half[:], 0.5)
 
-        pending = []
-        head = [0]
-        nquad = [0]
-
-        def emit_wacc(count):
-            for unused in range(min(count, len(pending) - head[0])):
-                ct, wcol, st, on_pe = pending[head[0]]
-                head[0] += 1
-                if on_pe:
-                    if st["npe"] == 0:
-                        st["ab"] = apool.tile([P, 512], F32, name="ab_acc", tag="ab")
-                    dg = dpool.tile([P, P], F32, tag="dg")
-                    nc.gpsimd.tensor_scalar(out=dg[:], in0=ident[:], scalar1=wcol, scalar2=0.0, op0=ALU.mult, op1=ALU.add)
-                    st["npe"] += 1
-                    nc.tensor.matmul(
-                        out=st["ab"][:], lhsT=dg[:], rhs=ct[:], start=(st["npe"] == 1), stop=(st["npe"] == st["pe_total"])
-                    )
-                elif st["nv"] == 0:
-                    st["o"] = work.tile([P, 512], F32, name="o_acc", tag="o")
-                    nc.vector.tensor_scalar(out=st["o"][:], in0=ct[:], scalar1=wcol, scalar2=None, op0=ALU.mult)
-                    st["nv"] += 1
-                else:
-                    nc.vector.scalar_tensor_tensor(
-                        out=st["o"][:], in0=ct[:], scalar=wcol, in1=st["o"][:], op0=ALU.mult, op1=ALU.add
-                    )
-                    st["nv"] += 1
-                if st["nv"] + st["npe"] == st["total"]:
-                    if st["pe_total"] > 0:
-                        nc.vector.tensor_tensor(out=st["o"][:], in0=st["ab"][:], in1=st["o"][:], op=ALU.add)
-                    for r in range(4):
-                        nc.sync.dma_start(out=out[:, 4 * st["m"] + r, :], in_=st["o"][32 * r : 32 * r + 32, :])
-
-        for m in range(7, -1, -1):
-            nd = 4 * (m + 1)
+        quads = []
+        for m in BLOCKS:
             tiles = [(d0, kap) for d0 in range(4) for kap in range(m + 1)]
-            ssq = small.tile([P, 32], F32, tag="ssq")
-            sc = small.tile([P, 32], F32, tag="sc")
-            cts = []
-            per_quad = -(-(len(pending) - head[0]) // (m + 1))
             for g in range(m + 1):
-                quad = tiles[4 * g : 4 * g + 4]
-                hp = work.tile([P, 2048], BF16, tag="hp")
-                for tq in range(4):
-                    zt = zpool.tile([P, 512], F32, name="zt", tag="z%d" % tq)
-                    for pos in range(4):
-                        d0, kap = quad[pos]
-                        cs = PADL + 128 * kap - 32 * d0
-                        if d0 % 2 == 0:
-                            xjc, xjs = ca, sa
-                        else:
-                            xjc, xjs = cb, sb
-                            cs -= 32
-                        ci = PADL + 128 * m
-                        zo = zt[:, 128 * pos : 128 * pos + 128]
-                        nc.tensor.matmul_mx(
-                            out=zo,
-                            lhsT=w1c[:, tq * 128 : tq * 128 + 128].bitcast(FP8X4),
-                            lhsT_scale=w1s[:, tq * 128 : tq * 128 + 128],
-                            rhs=ca[:, ci : ci + 128].bitcast(FP8X4),
-                            rhs_scale=sa[:, ci : ci + 128],
-                            start=True,
-                            stop=False,
-                        )
-                        nc.tensor.matmul_mx(
-                            out=zo,
-                            lhsT=w1c[:, 512 + tq * 128 : 512 + tq * 128 + 128].bitcast(FP8X4),
-                            lhsT_scale=w1s[:, 512 + tq * 128 : 512 + tq * 128 + 128],
-                            rhs=xjc[:, cs : cs + 128].bitcast(FP8X4),
-                            rhs_scale=xjs[:, cs : cs + 128],
-                            start=False,
-                            stop=True,
-                        )
-                    nc.scalar.activation(
-                        out=hp[:, tq * 512 : (tq + 1) * 512],
-                        in_=zt[:],
-                        func=ACT.Gelu,
-                        bias=b1f[:, tq : tq + 1],
-                        scale=1.0,
-                    )
-                hg = work.tile([P, 2048], BF16, tag="hg", align_bytes=64)
-                eng = REGROUP[nquad[0] % len(REGROUP)]
-                nquad[0] += 1
-                if eng == "V":
-                    nc.vector.tensor_copy(
-                        out=hg[:].rearrange("p (c i t) -> p c t i", i=4, t=4),
-                        in_=hp[:].rearrange("p (t c i) -> p c t i", t=4, i=4),
-                    )
-                elif eng == "S":
-                    nc.scalar.copy(
-                        out=hg[:].rearrange("p (c i t) -> p c t i", i=4, t=4),
-                        in_=hp[:].rearrange("p (t c i) -> p c t i", t=4, i=4),
-                    )
-                else:
-                    nc.gpsimd.tensor_scalar(
-                        out=hg[:].rearrange("p (c t) -> p c t", t=4),
-                        in0=hp[:].rearrange("p (t c) -> p c t", t=4),
-                        scalar1=1.0,
-                        scalar2=0.0,
-                        op0=ALU.mult,
-                        op1=ALU.add,
-                    )
-                hc = work.tile([P, 512], U32, tag="hc", align_bytes=64)
-                hs = work.tile([P, 512], U8, tag="hs", align_bytes=64)
-                nc.vector.quantize_mx(out=hc[:].bitcast(FP8X4), scales=hs[:], in_=hg[:])
+                quads.append({"m": m, "g": g, "tiles": tiles[4 * g : 4 * g + 4], "last": g == m})
+        nq = len(quads)
+        blk = {}
+        for m in BLOCKS:
+            blk[m] = {"m": m, "nd": 4 * (m + 1), "cts": [], "nv": 0, "npe": 0, "fin": False}
+        pend_v = []
+        pend_p = []
+        head = {"v": 0, "p": 0, "live": 0}
+        fin_q = []
+
+        def emit_z(k, banks):
+            if k >= nq:
+                return
+            q = quads[k]
+            m = q["m"]
+            if "zt" not in q:
+                q["zt"] = {}
+            ci = PADL + 128 * m
+            for tq in banks:
+                zt = zpool.tile([P, 512], F32, name="zt", tag="z%d" % tq)
+                q["zt"][tq] = zt
                 for pos in range(4):
-                    d0, kap = quad[pos]
-                    col = 4 * g + pos
-                    pp = ppool.tile([P, 512], F32, tag="pp")
+                    d0, kap = q["tiles"][pos]
+                    cs = PADL + 128 * kap - 32 * d0
+                    if d0 % 2 == 0:
+                        xjc, xjs = ca, sa
+                    else:
+                        xjc, xjs = cb, sb
+                        cs -= 32
+                    zo = zt[:, 128 * pos : 128 * pos + 128]
                     nc.tensor.matmul_mx(
-                        out=pp[:],
-                        lhsT=hc[:, 128 * pos : 128 * pos + 128].bitcast(FP8X4),
-                        lhsT_scale=hs[:, 128 * pos : 128 * pos + 128],
-                        rhs=w2c[:].bitcast(FP8X4),
-                        rhs_scale=w2s[:],
+                        out=zo,
+                        lhsT=w1c[:, tq * 128 : tq * 128 + 128].bitcast(FP8X4),
+                        lhsT_scale=w1s[:, tq * 128 : tq * 128 + 128],
+                        rhs=ca[:, ci : ci + 128].bitcast(FP8X4),
+                        rhs_scale=sa[:, ci : ci + 128],
                         start=True,
+                        stop=False,
+                    )
+                    nc.tensor.matmul_mx(
+                        out=zo,
+                        lhsT=w1c[:, 512 + tq * 128 : 512 + tq * 128 + 128].bitcast(FP8X4),
+                        lhsT_scale=w1s[:, 512 + tq * 128 : 512 + tq * 128 + 128],
+                        rhs=xjc[:, cs : cs + 128].bitcast(FP8X4),
+                        rhs_scale=xjs[:, cs : cs + 128],
+                        start=False,
                         stop=True,
                     )
-                    ct = cpool.tile([P, 512], F32, tag="c")
-                    nc.vector.tensor_tensor(out=ct[:], in0=pp[:], in1=b2b[:], op=ALU.add)
-                    junk = work.tile([P, 512], BF16, tag="junk")
-                    nc.scalar.activation(out=junk[:], in_=ct[:], func=ACT.Square, accum_out=ssq[:, col : col + 1])
-                    cts.append((ct, col))
-                nc.gpsimd.tensor_tensor(out=sc[:, 4 * g : 4 * g + 4], in0=ssq[:, 4 * g : 4 * g + 4], in1=half[:], op=ALU.pow)
-                emit_wacc(per_quad)
-            emit_wacc(len(pending))
-            sk = small.tile([P, 32], F32, tag="sk")
-            nc.vector.tensor_tensor(out=sk[:, 0:nd], in0=sc[:, 0:nd], in1=negm[:, 32 * m : 32 * m + nd], op=ALU.add)
-            mx = small.tile([P, 1], F32, tag="mx")
+
+        def emit_regroup(k, engine):
+            q = quads[k]
+            hg = work.tile([P, 2048], BF16, name="hg", tag="hg", align_bytes=64)
+            q["hg"] = hg
+            dst = hg[:].rearrange("p (c i t) -> p c t i", i=4, t=4)
+            src = q["hp"][:].rearrange("p (t c i) -> p c t i", t=4, i=4)
+            if engine == "S":
+                nc.scalar.copy(out=dst, in_=src)
+            else:
+                nc.vector.tensor_copy(out=dst, in_=src)
+
+        def emit_gelu(k):
+            if k >= nq:
+                return
+            q = quads[k]
+            hp = work.tile([P, 2048], BF16, name="hp", tag="hp")
+            q["hp"] = hp
+            for tq in range(4):
+                nc.scalar.activation(
+                    out=hp[:, tq * 512 : (tq + 1) * 512],
+                    in_=q["zt"][tq][:],
+                    func=ACT.Gelu,
+                    bias=b1f[:, tq : tq + 1],
+                    scale=1.0,
+                )
+            if regroup_on_scalar(k):
+                emit_regroup(k, "S")
+
+        def emit_quant(k):
+            q = quads[k]
+            if not regroup_on_scalar(k):
+                emit_regroup(k, "V")
+            hc = work.tile([P, 512], U32, name="hc", tag="hc", align_bytes=64)
+            hs = work.tile([P, 512], U8, name="hs", tag="hs", align_bytes=64)
+            q["hc"] = hc
+            q["hs"] = hs
+            q["pp"] = {}
+            q["ct"] = {}
+            nc.vector.quantize_mx(out=hc[:].bitcast(FP8X4), scales=hs[:], in_=q["hg"][:])
+
+        def emit_s2(k, pos):
+            q = quads[k]
+            pp = ppool.tile([P, 512], F32, name="pp", tag="pp")
+            q["pp"][pos] = pp
+            nc.tensor.matmul_mx(
+                out=pp[:],
+                lhsT=q["hc"][:, 128 * pos : 128 * pos + 128].bitcast(FP8X4),
+                lhsT_scale=q["hs"][:, 128 * pos : 128 * pos + 128],
+                rhs=w2c[:].bitcast(FP8X4),
+                rhs_scale=w2s[:],
+                start=True,
+                stop=True,
+            )
+
+        def emit_evac(k, pos):
+            q = quads[k]
+            ct = cpool.tile([P, 512], F32, name="ct", tag="c")
+            head["live"] += 1
+            assert head["live"] <= NC_RING
+            q["ct"][pos] = ct
+            nc.vector.tensor_tensor(out=ct[:], in0=q["pp"][pos][:], in1=b2b[:], op=ALU.add)
+
+        def emit_square(k):
+            q = quads[k]
+            st = blk[q["m"]]
+            g = q["g"]
+            if g == 0:
+                st["ssq"] = small.tile([P, 32], F32, name="ssq", tag="ssq")
+                st["sc"] = small.tile([P, 32], F32, name="sc", tag="sc")
+            for pos in range(4):
+                col = 4 * g + pos
+                junk = work.tile([P, 512], BF16, name="junk", tag="junk")
+                nc.scalar.activation(
+                    out=junk[:], in_=q["ct"][pos][:], func=ACT.Square, accum_out=st["ssq"][:, col : col + 1]
+                )
+                st["cts"].append(q["ct"][pos])
+            nc.gpsimd.tensor_tensor(
+                out=st["sc"][:, 4 * g : 4 * g + 4], in0=st["ssq"][:, 4 * g : 4 * g + 4], in1=half[:], op=ALU.pow
+            )
+
+        def emit_softmax_a(m):
+            st = blk[m]
+            nd = st["nd"]
+            sk = small.tile([P, 32], F32, name="sk", tag="sk")
+            nc.vector.tensor_tensor(out=sk[:, 0:nd], in0=st["sc"][:, 0:nd], in1=negm[:, 32 * m : 32 * m + nd], op=ALU.add)
+            mx = small.tile([P, 1], F32, name="mx", tag="mx")
             nc.vector.tensor_reduce(out=mx[:], in_=sk[:, 0:nd], axis=AX.X, op=ALU.max)
-            nh = small.tile([P, 1], F32, tag="nh")
+            nh = small.tile([P, 1], F32, name="nh", tag="nh")
             nc.vector.tensor_scalar(out=nh[:], in0=mx[:], scalar1=-0.5, scalar2=None, op0=ALU.mult)
-            th = small.tile([P, 32], F32, tag="th")
-            nc.scalar.activation(out=th[:, 0:nd], in_=sk[:, 0:nd], func=ACT.Tanh, bias=nh[:, 0:1], scale=0.5)
-            bq = small.tile([P, 32], F32, tag="bq")
+            st["sk"] = sk
+            st["nh"] = nh
+
+        def emit_tanh(m):
+            st = blk[m]
+            nd = st["nd"]
+            th = small.tile([P, 32], F32, name="th", tag="th")
+            nc.scalar.activation(out=th[:, 0:nd], in_=st["sk"][:, 0:nd], func=ACT.Tanh, bias=st["nh"][:, 0:1], scale=0.5)
+            st["th"] = th
+
+        def emit_softmax_b(m):
+            st = blk[m]
+            nd = st["nd"]
+            th = st["th"]
+            bq = small.tile([P, 32], F32, name="bq", tag="bq")
             nc.vector.tensor_scalar(out=bq[:, 0:nd], in0=th[:, 0:nd], scalar1=-1.0, scalar2=1.0, op0=ALU.mult, op1=ALU.add)
-            rb = small.tile([P, 32], F32, tag="rb")
+            rb = small.tile([P, 32], F32, name="rb", tag="rb")
             nc.vector.reciprocal(out=rb[:, 0:nd], in_=bq[:, 0:nd])
-            ex = small.tile([P, 32], F32, tag="ex")
-            se = small.tile([P, 1], F32, tag="se")
+            ex = small.tile([P, 32], F32, name="ex", tag="ex")
+            se = small.tile([P, 1], F32, name="se", tag="se")
             nc.vector.scalar_tensor_tensor(
                 out=ex[:, 0:nd], in0=th[:, 0:nd], scalar=1.0, in1=rb[:, 0:nd], op0=ALU.add, op1=ALU.mult, accum_out=se[:]
             )
-            rs = small.tile([P, 1], F32, tag="rs")
+            rs = small.tile([P, 1], F32, name="rs", tag="rs")
             nc.vector.reciprocal(out=rs[:], in_=se[:])
-            wt = small.tile([P, 32], F32, tag="wt")
+            wt = small.tile([P, 32], F32, name="wt", tag="wt")
             nc.vector.tensor_scalar(out=wt[:, 0:nd], in0=ex[:, 0:nd], scalar1=rs[:, 0:1], scalar2=None, op0=ALU.mult)
-            npe = N_PE[m]
-            st = {"nv": 0, "npe": 0, "total": nd, "pe_total": npe, "m": m, "o": None, "ab": None}
-            for idx in range(nd):
-                ct, col = cts[idx]
-                on_pe = ((idx + 1) * npe) // nd > (idx * npe) // nd and idx > 0
-                pending.append((ct, wt[:, col : col + 1], st, on_pe))
-        emit_wacc(len(pending))
+            st["wt"] = wt
+            for col in range(nd):
+                if col < nd - N_PE[m]:
+                    pend_v.append((m, col))
+                else:
+                    pend_p.append((m, col))
+
+        def note_done(st):
+            head["live"] -= 1
+            if st["nv"] + st["npe"] == st["nd"]:
+                fin_q.append((st["m"], head["k"]))
+
+        def emit_wacc_v(count):
+            for unused in range(min(count, len(pend_v) - head["v"])):
+                m, col = pend_v[head["v"]]
+                head["v"] += 1
+                st = blk[m]
+                wcol = st["wt"][:, col : col + 1]
+                if st["nv"] == 0:
+                    st["o"] = work.tile([P, 512], F32, name="o_acc", tag="o")
+                    nc.vector.tensor_scalar(out=st["o"][:], in0=st["cts"][col][:], scalar1=wcol, scalar2=None, op0=ALU.mult)
+                else:
+                    nc.vector.scalar_tensor_tensor(
+                        out=st["o"][:], in0=st["cts"][col][:], scalar=wcol, in1=st["o"][:], op0=ALU.mult, op1=ALU.add
+                    )
+                st["nv"] += 1
+                note_done(st)
+
+        def emit_wacc_p(count):
+            for unused in range(min(count, len(pend_p) - head["p"])):
+                m, col = pend_p[head["p"]]
+                st = blk[m]
+                if st["npe"] == 0:
+                    if head["ab_busy"]:
+                        return
+                    head["ab_busy"] = True
+                    st["ab"] = apool.tile([P, 512], F32, name="ab_acc", tag="ab")
+                head["p"] += 1
+                dg = dpool.tile([P, P], F32, name="dg", tag="dg")
+                nc.gpsimd.tensor_scalar(
+                    out=dg[:], in0=ident[:], scalar1=st["wt"][:, col : col + 1], scalar2=0.0, op0=ALU.mult, op1=ALU.add
+                )
+                st["npe"] += 1
+                nc.tensor.matmul(
+                    out=st["ab"][:], lhsT=dg[:], rhs=st["cts"][col][:], start=(st["npe"] == 1), stop=(st["npe"] == N_PE[m])
+                )
+                note_done(st)
+
+        def emit_fin(force):
+            while len(fin_q) > head["f"] and (force or fin_q[head["f"]][1] < head["k"]):
+                m = fin_q[head["f"]][0]
+                head["f"] += 1
+                st = blk[m]
+                nc.vector.tensor_tensor(out=st["o"][:], in0=st["ab"][:], in1=st["o"][:], op=ALU.add)
+                head["ab_busy"] = False
+                for r in range(4):
+                    nc.sync.dma_start(out=out[:, 4 * m + r, :], in_=st["o"][32 * r : 32 * r + 32, :])
+
+        head["k"] = 0
+        head["f"] = 0
+        head["ab_busy"] = False
+        if MANUAL:
+            ctx.enter_context(tc.manual_schedule())
+        when_a = {}
+        when_t = {}
+        when_b = {}
+        emit_z(0, (0, 1, 2, 3))
+        emit_gelu(0)
+        emit_z(1, (0, 1, 2, 3))
+        for k in range(nq + 5):
+            head["k"] = k
+            live = k < nq
+            if live:
+                emit_quant(k)
+                emit_gelu(k + 1)
+            if k in when_t:
+                emit_tanh(when_t[k])
+            if live:
+                emit_s2(k, 0)
+                emit_s2(k, 1)
+                emit_s2(k, 2)
+                emit_z(k + 2, (0, 1))
+            emit_wacc_v(NV if live else 1000)
+            if k in when_b:
+                emit_softmax_b(when_b[k])
+            emit_fin(not live)
+            if live:
+                emit_evac(k, 0)
+                emit_s2(k, 3)
+                emit_z(k + 2, (2, 3))
+            emit_wacc_p(NP if live else 1000)
+            if live:
+                emit_evac(k, 1)
+                emit_evac(k, 2)
+                emit_evac(k, 3)
+                emit_square(k)
+            if k in when_a:
+                emit_softmax_a(when_a[k])
+            if live and quads[k]["last"]:
+                when_a[k + 1] = quads[k]["m"]
+                when_t[k + 2] = quads[k]["m"]
+                when_b[k + 2] = quads[k]["m"]
+        assert head["v"] == len(pend_v) and head["p"] == len(pend_p) and head["f"] == 8

@@ -21,9 +21,8 @@ NEG = -1.0e9
 NC_RING = 52
 N_PE = (2, 3, 5, 6, 8, 10, 11, 13)
 BLOCKS = (7, 6, 5, 4, 3, 2, 1, 0)
-NV = 3
-NP = 2
-MANUAL = True
+LAG = 2
+RATE = 6
 
 
 def regroup_on_scalar(k):
@@ -37,7 +36,7 @@ def tile_pairconnect_kernel(tc, x, W1, b1, W2, b2, out):
         pro = ctx.enter_context(tc.tile_pool(name="pro", bufs=1))
         work = ctx.enter_context(tc.tile_pool(name="work", bufs=3))
         cpool = ctx.enter_context(tc.tile_pool(name="cring", bufs=NC_RING))
-        small = ctx.enter_context(tc.tile_pool(name="small", bufs=3))
+        small = ctx.enter_context(tc.tile_pool(name="small", bufs=5))
         dpool = ctx.enter_context(tc.tile_pool(name="diag", bufs=4))
         zpool = ctx.enter_context(tc.psum_pool(name="zps", bufs=1))
         ppool = ctx.enter_context(tc.psum_pool(name="pps", bufs=3))
@@ -132,7 +131,7 @@ def tile_pairconnect_kernel(tc, x, W1, b1, W2, b2, out):
             for d0 in range(1, 4):
                 c = 32 * m + d0 * (m + 1)
                 nc.gpsimd.memset(negm[0 : 32 * d0, c : c + 1], NEG)
-        half = const.tile([P, 4], F32)
+        half = const.tile([P, 32], F32)
         nc.gpsimd.memset(half[:], 0.5)
 
         quads = []
@@ -144,10 +143,8 @@ def tile_pairconnect_kernel(tc, x, W1, b1, W2, b2, out):
         blk = {}
         for m in BLOCKS:
             blk[m] = {"m": m, "nd": 4 * (m + 1), "cts": [], "nv": 0, "npe": 0, "fin": False}
-        pend_v = []
-        pend_p = []
-        head = {"v": 0, "p": 0, "live": 0}
-        fin_q = []
+        pend = []
+        head = {"w": 0, "live": 0, "k": 0}
 
         def emit_z(k, banks):
             if k >= nq:
@@ -264,13 +261,11 @@ def tile_pairconnect_kernel(tc, x, W1, b1, W2, b2, out):
                     out=junk[:], in_=q["ct"][pos][:], func=ACT.Square, accum_out=st["ssq"][:, col : col + 1]
                 )
                 st["cts"].append(q["ct"][pos])
-            nc.gpsimd.tensor_tensor(
-                out=st["sc"][:, 4 * g : 4 * g + 4], in0=st["ssq"][:, 4 * g : 4 * g + 4], in1=half[:], op=ALU.pow
-            )
 
         def emit_softmax_a(m):
             st = blk[m]
             nd = st["nd"]
+            nc.gpsimd.tensor_tensor(out=st["sc"][:, 0:nd], in0=st["ssq"][:, 0:nd], in1=half[:, 0:nd], op=ALU.pow)
             sk = small.tile([P, 32], F32, name="sk", tag="sk")
             nc.vector.tensor_tensor(out=sk[:, 0:nd], in0=st["sc"][:, 0:nd], in1=negm[:, 32 * m : 32 * m + nd], op=ALU.add)
             mx = small.tile([P, 1], F32, name="mx", tag="mx")
@@ -305,105 +300,57 @@ def tile_pairconnect_kernel(tc, x, W1, b1, W2, b2, out):
             wt = small.tile([P, 32], F32, name="wt", tag="wt")
             nc.vector.tensor_scalar(out=wt[:, 0:nd], in0=ex[:, 0:nd], scalar1=rs[:, 0:1], scalar2=None, op0=ALU.mult)
             st["wt"] = wt
+            npe = N_PE[m]
             for col in range(nd):
-                if col < nd - N_PE[m]:
-                    pend_v.append((m, col))
-                else:
-                    pend_p.append((m, col))
+                on_pe = ((col + 1) * npe) // nd > (col * npe) // nd
+                pend.append((m, col, on_pe, head["k"]))
 
-        def note_done(st):
-            head["live"] -= 1
-            if st["nv"] + st["npe"] == st["nd"]:
-                fin_q.append((st["m"], head["k"]))
-
-        def emit_wacc_v(count):
-            for unused in range(min(count, len(pend_v) - head["v"])):
-                m, col = pend_v[head["v"]]
-                head["v"] += 1
+        def emit_wacc(count, k_now):
+            for unused in range(count):
+                if head["w"] >= len(pend) or pend[head["w"]][3] + LAG > k_now:
+                    return
+                m, col, on_pe, unused_k = pend[head["w"]]
+                head["w"] += 1
                 st = blk[m]
                 wcol = st["wt"][:, col : col + 1]
-                if st["nv"] == 0:
+                ct = st["cts"][col]
+                if on_pe:
+                    if st["npe"] == 0:
+                        st["ab"] = apool.tile([P, 512], F32, name="ab_acc", tag="ab")
+                    dg = dpool.tile([P, P], F32, name="dg", tag="dg")
+                    nc.scalar.activation(out=dg[:], in_=ident[:], func=ACT.Copy, scale=wcol)
+                    st["npe"] += 1
+                    nc.tensor.matmul(
+                        out=st["ab"][:], lhsT=dg[:], rhs=ct[:], start=(st["npe"] == 1), stop=(st["npe"] == N_PE[m])
+                    )
+                elif st["nv"] == 0:
                     st["o"] = work.tile([P, 512], F32, name="o_acc", tag="o")
-                    nc.vector.tensor_scalar(out=st["o"][:], in0=st["cts"][col][:], scalar1=wcol, scalar2=None, op0=ALU.mult)
+                    nc.vector.tensor_scalar(out=st["o"][:], in0=ct[:], scalar1=wcol, scalar2=None, op0=ALU.mult)
+                    st["nv"] += 1
                 else:
                     nc.vector.scalar_tensor_tensor(
-                        out=st["o"][:], in0=st["cts"][col][:], scalar=wcol, in1=st["o"][:], op0=ALU.mult, op1=ALU.add
+                        out=st["o"][:], in0=ct[:], scalar=wcol, in1=st["o"][:], op0=ALU.mult, op1=ALU.add
                     )
-                st["nv"] += 1
-                note_done(st)
+                    st["nv"] += 1
+                head["live"] -= 1
+                if st["nv"] + st["npe"] == st["nd"]:
+                    nc.vector.tensor_tensor(out=st["o"][:], in0=st["ab"][:], in1=st["o"][:], op=ALU.add)
+                    for r in range(4):
+                        nc.sync.dma_start(out=out[:, 4 * m + r, :], in_=st["o"][32 * r : 32 * r + 32, :])
 
-        def emit_wacc_p(count):
-            for unused in range(min(count, len(pend_p) - head["p"])):
-                m, col = pend_p[head["p"]]
-                st = blk[m]
-                if st["npe"] == 0:
-                    if head["ab_busy"]:
-                        return
-                    head["ab_busy"] = True
-                    st["ab"] = apool.tile([P, 512], F32, name="ab_acc", tag="ab")
-                head["p"] += 1
-                dg = dpool.tile([P, P], F32, name="dg", tag="dg")
-                nc.gpsimd.tensor_scalar(
-                    out=dg[:], in0=ident[:], scalar1=st["wt"][:, col : col + 1], scalar2=0.0, op0=ALU.mult, op1=ALU.add
-                )
-                st["npe"] += 1
-                nc.tensor.matmul(
-                    out=st["ab"][:], lhsT=dg[:], rhs=st["cts"][col][:], start=(st["npe"] == 1), stop=(st["npe"] == N_PE[m])
-                )
-                note_done(st)
-
-        def emit_fin(force):
-            while len(fin_q) > head["f"] and (force or fin_q[head["f"]][1] < head["k"]):
-                m = fin_q[head["f"]][0]
-                head["f"] += 1
-                st = blk[m]
-                nc.vector.tensor_tensor(out=st["o"][:], in0=st["ab"][:], in1=st["o"][:], op=ALU.add)
-                head["ab_busy"] = False
-                for r in range(4):
-                    nc.sync.dma_start(out=out[:, 4 * m + r, :], in_=st["o"][32 * r : 32 * r + 32, :])
-
-        head["k"] = 0
-        head["f"] = 0
-        head["ab_busy"] = False
-        if MANUAL:
-            ctx.enter_context(tc.manual_schedule())
-        when_a = {}
-        when_t = {}
-        when_b = {}
-        emit_z(0, (0, 1, 2, 3))
-        emit_gelu(0)
-        emit_z(1, (0, 1, 2, 3))
-        for k in range(nq + 5):
+        for k in range(nq):
             head["k"] = k
-            live = k < nq
-            if live:
-                emit_quant(k)
-                emit_gelu(k + 1)
-            if k in when_t:
-                emit_tanh(when_t[k])
-            if live:
-                emit_s2(k, 0)
-                emit_s2(k, 1)
-                emit_s2(k, 2)
-                emit_z(k + 2, (0, 1))
-            emit_wacc_v(NV if live else 1000)
-            if k in when_b:
-                emit_softmax_b(when_b[k])
-            emit_fin(not live)
-            if live:
-                emit_evac(k, 0)
-                emit_s2(k, 3)
-                emit_z(k + 2, (2, 3))
-            emit_wacc_p(NP if live else 1000)
-            if live:
-                emit_evac(k, 1)
-                emit_evac(k, 2)
-                emit_evac(k, 3)
-                emit_square(k)
-            if k in when_a:
-                emit_softmax_a(when_a[k])
-            if live and quads[k]["last"]:
-                when_a[k + 1] = quads[k]["m"]
-                when_t[k + 2] = quads[k]["m"]
-                when_b[k + 2] = quads[k]["m"]
-        assert head["v"] == len(pend_v) and head["p"] == len(pend_p) and head["f"] == 8
+            emit_z(k, (0, 1, 2, 3))
+            emit_gelu(k)
+            emit_quant(k)
+            for pos in range(4):
+                emit_s2(k, pos)
+                emit_evac(k, pos)
+            emit_square(k)
+            if quads[k]["last"]:
+                emit_softmax_a(quads[k]["m"])
+                emit_tanh(quads[k]["m"])
+                emit_softmax_b(quads[k]["m"])
+            emit_wacc(RATE, k)
+        emit_wacc(1000, nq + LAG)
+        assert head["w"] == 144

@@ -9,6 +9,7 @@ F32 = mybir.dt.float32
 BF16 = mybir.dt.bfloat16
 U32 = mybir.dt.uint32
 U8 = mybir.dt.uint8
+I32 = mybir.dt.int32
 FP8X4 = mybir.dt.float8_e4m3fn_x4
 ALU = mybir.AluOpType
 ACT = mybir.ActivationFunctionType
@@ -33,106 +34,123 @@ def tile_pairconnect_kernel(tc, x, W1, b1, W2, b2, out):
     nc = tc.nc
     with ExitStack() as ctx:
         const = ctx.enter_context(tc.tile_pool(name="const", bufs=1))
-        pro = ctx.enter_context(tc.tile_pool(name="pro", bufs=1))
         work = ctx.enter_context(tc.tile_pool(name="work", bufs=3))
-        cpool = ctx.enter_context(tc.tile_pool(name="cring", bufs=NC_RING))
         small = ctx.enter_context(tc.tile_pool(name="small", bufs=5))
         dpool = ctx.enter_context(tc.tile_pool(name="diag", bufs=4))
         zpool = ctx.enter_context(tc.psum_pool(name="zps", bufs=1))
         ppool = ctx.enter_context(tc.psum_pool(name="pps", bufs=3))
         apool = ctx.enter_context(tc.psum_pool(name="aps", bufs=1))
 
-        xr = pro.tile([P, 4096], BF16)
-        xv = x.flatten_outer_dims().rearrange("(n p) k -> p n k", p=P)
-        xrv = xr[:].rearrange("p (n k) -> p n k", n=8)
-        nc.sync.dma_start(out=xrv[:, 0:4, :], in_=xv[:, 0:4, :])
-        nc.sync.dma_start(out=xrv[:, 4:8, :], in_=xv[:, 4:8, :])
-        w1r = pro.tile([P, 4096], BF16)
-        nc.sync.dma_start(
-            out=w1r[:].rearrange("p (a f) -> p a f", a=4),
-            in_=W1.rearrange("(a q e) c -> q a (e c)", a=4, q=P, e=2),
-        )
-        w2r = pro.tile([P, 2048], BF16)
-        nc.sync.dma_start(
-            out=w2r[:].rearrange("p (t n) -> p t n", t=4),
-            in_=W2.rearrange("(p t) n -> p t n", t=4),
-        )
-        b1r = pro.tile([P, 4], BF16)
-        nc.sync.dma_start(out=b1r[:], in_=b1.rearrange("(p t) -> p t", t=4))
-        b2r = pro.tile([P, 512], BF16)
-        nc.sync.dma_start(out=b2r[:], in_=b2.partition_broadcast(P))
-
-        ident = const.tile([P, P], F32)
-        make_identity(nc, ident[:])
-
-        xg = pro.tile([P, NCOL * 4], BF16, align_bytes=64)
-        xg32 = xg[:].bitcast(F32)
-        nc.vector.memset(xg32[:, 0 : 2 * PADL], 0.0)
-        nc.vector.memset(xg32[:, 2 * (PADL + 1024) : 2 * NCOL], 0.0)
-        xr32 = xr[:].bitcast(F32)
-        xbody = xg32[:, 2 * PADL : 2 * PADL + 2048].rearrange(
-            "p (i b u) -> p i b u", i=32, b=32, u=2
-        )
-        for j in range(4):
-            pt = ppool.tile([P, 512], F32, tag="pp")
-            for u in range(2):
-                for n2 in range(2):
-                    off = u * 256 + n2 * 128
-                    src0 = (2 * j + n2) * 256 + u * 128
-                    nc.tensor.transpose(pt[:, off : off + 128], xr32[:, src0 : src0 + 128], ident[:])
-            src = pt[:].rearrange("p (u c i) -> p i c u", u=2, c=8, i=32)
-            dst = xbody[:, :, 8 * j : 8 * j + 8, :]
-            if j % 2 == 0:
-                nc.vector.tensor_copy(out=dst, in_=src)
-            else:
-                nc.scalar.copy(out=dst, in_=src)
-
-        ca = const.tile([P, 1152], U32, align_bytes=64)
-        sa = const.tile([P, 1152], U8, align_bytes=64)
-        cb = const.tile([P, 1152], U32, align_bytes=64)
-        sb = const.tile([P, 1152], U8, align_bytes=64)
-
-        w1g = pro.tile([P, 4096], BF16, align_bytes=64)
-        w1c = const.tile([P, 1024], U32, align_bytes=64)
-        w1s = const.tile([P, 1024], U8, align_bytes=64)
-        for h in range(2):
-            dst = w1g[:, h * 2048 : (h + 1) * 2048].rearrange("p (q m t) -> p q m t", q=4, m=P, t=4)
-            src = w1r[:, h * 2048 : (h + 1) * 2048].rearrange("p (t m q) -> p q m t", t=4, m=P, q=4)
-            if h == 0:
-                nc.vector.tensor_copy(out=dst, in_=src)
-            else:
-                nc.scalar.copy(out=dst, in_=src)
-        nc.vector.quantize_mx(out=ca[:, 0:1024].bitcast(FP8X4), scales=sa[:, 0:1024], in_=xg[:, 0:4096])
-        nc.vector.quantize_mx(out=ca[:, 1024:1152].bitcast(FP8X4), scales=sa[:, 1024:1152], in_=xg[:, 4096:4608])
-        for h in range(2):
-            nc.vector.quantize_mx(
-                out=w1c[:, h * 512 : (h + 1) * 512].bitcast(FP8X4),
-                scales=w1s[:, h * 512 : (h + 1) * 512],
-                in_=w1g[:, h * 2048 : (h + 1) * 2048],
+        with tc.tile_pool(name="pro", bufs=1) as pro:
+            xr = pro.tile([P, 4096], BF16)
+            xv = x.flatten_outer_dims().rearrange("(n p) k -> p n k", p=P)
+            xrv = xr[:].rearrange("p (n k) -> p n k", n=8)
+            nc.sync.dma_start(out=xrv[:, 0:4, :], in_=xv[:, 0:4, :])
+            nc.sync.dma_start(out=xrv[:, 4:8, :], in_=xv[:, 4:8, :])
+            w1r = pro.tile([P, 4096], BF16)
+            nc.sync.dma_start(
+                out=w1r[:].rearrange("p (a f) -> p a f", a=4),
+                in_=W1.rearrange("(a q e) c -> q a (e c)", a=4, q=P, e=2),
             )
-        b1f = const.tile([P, 4], F32)
-        nc.vector.tensor_copy(out=b1f[:], in_=b1r[:])
-        nc.vector.quantize_mx(out=cb[:, 0:1024].bitcast(FP8X4), scales=sb[:, 0:1024], in_=xg[:, 128:4224])
-        nc.vector.quantize_mx(out=cb[:, 1024:1152].bitcast(FP8X4), scales=sb[:, 1024:1152], in_=xg[:, 4224:4736])
+            w2r = pro.tile([P, 2048], BF16)
+            nc.sync.dma_start(
+                out=w2r[:].rearrange("p (t n) -> p t n", t=4),
+                in_=W2.rearrange("(p t) n -> p t n", t=4),
+            )
+            b1r = pro.tile([P, 4], BF16)
+            nc.sync.dma_start(out=b1r[:], in_=b1.rearrange("(p t) -> p t", t=4))
+            b2r = pro.tile([P, 512], BF16)
+            nc.sync.dma_start(out=b2r[:], in_=b2.partition_broadcast(P))
 
-        w2g = pro.tile([P, 2048], BF16, align_bytes=64)
-        w2c = const.tile([P, 512], U32, align_bytes=64)
-        w2s = const.tile([P, 512], U8, align_bytes=64)
-        nc.scalar.copy(
-            out=w2g[:].rearrange("p (n t) -> p n t", t=4),
-            in_=w2r[:].rearrange("p (t n) -> p n t", t=4),
-        )
-        nc.vector.quantize_mx(out=w2c[:].bitcast(FP8X4), scales=w2s[:], in_=w2g[:])
-        b2b = const.tile([P, 512], F32)
-        nc.gpsimd.tensor_copy(out=b2b[:], in_=b2r[:])
-        negm = const.tile([P, 8 * 32], F32)
-        nc.gpsimd.memset(negm[:], 0.0)
-        for m in range(8):
-            for d0 in range(1, 4):
-                c = 32 * m + d0 * (m + 1)
-                nc.gpsimd.memset(negm[0 : 32 * d0, c : c + 1], NEG)
-        half = const.tile([P, 32], F32)
-        nc.gpsimd.memset(half[:], 0.5)
+            ident = const.tile([P, P], F32)
+            make_identity(nc, ident[:])
+
+            xg = pro.tile([P, NCOL * 4], BF16, align_bytes=64)
+            xg32 = xg[:].bitcast(F32)
+            nc.vector.memset(xg32[:, 0 : 2 * PADL], 0.0)
+            nc.vector.memset(xg32[:, 2 * (PADL + 1024) : 2 * NCOL], 0.0)
+            xr32 = xr[:].bitcast(F32)
+            xbody = xg32[:, 2 * PADL : 2 * PADL + 2048].rearrange(
+                "p (i b u) -> p i b u", i=32, b=32, u=2
+            )
+            for j in range(4):
+                pt = ppool.tile([P, 512], F32, tag="pp")
+                for u in range(2):
+                    for n2 in range(2):
+                        off = u * 256 + n2 * 128
+                        src0 = (2 * j + n2) * 256 + u * 128
+                        nc.tensor.transpose(pt[:, off : off + 128], xr32[:, src0 : src0 + 128], ident[:])
+                src = pt[:].rearrange("p (u c i) -> p i c u", u=2, c=8, i=32)
+                dst = xbody[:, :, 8 * j : 8 * j + 8, :]
+                if j % 2 == 0:
+                    nc.vector.tensor_copy(out=dst, in_=src)
+                else:
+                    nc.scalar.copy(out=dst, in_=src)
+
+            ca = const.tile([P, 1152], U32, align_bytes=64)
+            sa = const.tile([P, 1152], U8, align_bytes=64)
+            cb = const.tile([P, 1152], U32, align_bytes=64)
+            sb = const.tile([P, 1152], U8, align_bytes=64)
+
+            w1g = pro.tile([P, 4096], BF16, align_bytes=64)
+            w1c = const.tile([P, 1024], U32, align_bytes=64)
+            w1s = const.tile([P, 1024], U8, align_bytes=64)
+            for h in range(2):
+                dst = w1g[:, h * 2048 : (h + 1) * 2048].rearrange("p (q m t) -> p q m t", q=4, m=P, t=4)
+                src = w1r[:, h * 2048 : (h + 1) * 2048].rearrange("p (t m q) -> p q m t", t=4, m=P, q=4)
+                if h == 0:
+                    nc.vector.tensor_copy(out=dst, in_=src)
+                else:
+                    nc.scalar.copy(out=dst, in_=src)
+            nc.vector.quantize_mx(out=ca[:, 0:1024].bitcast(FP8X4), scales=sa[:, 0:1024], in_=xg[:, 0:4096])
+            nc.vector.quantize_mx(out=ca[:, 1024:1152].bitcast(FP8X4), scales=sa[:, 1024:1152], in_=xg[:, 4096:4608])
+            xic = const.tile([P, 8 * 512], U32, align_bytes=64)
+            xis = const.tile([P, 8 * 512], U8, align_bytes=64)
+
+            def replicate(m):
+                ci = PADL + 128 * m
+                nc.vector.tensor_copy(
+                    out=xic[:, 512 * m : 512 * m + 512].bitcast(I32).rearrange("p (r w) -> p r w", r=4),
+                    in_=ca[:, ci : ci + 128].bitcast(I32).unsqueeze(1).to_broadcast([P, 4, 128]),
+                )
+                nc.vector.tensor_copy(
+                    out=xis[:, 512 * m : 512 * m + 512].bitcast(I32).rearrange("p (r w) -> p r w", r=4),
+                    in_=sa[:, ci : ci + 128].bitcast(I32).unsqueeze(1).to_broadcast([P, 4, 32]),
+                )
+
+            replicate(BLOCKS[0])
+            for h in range(2):
+                nc.vector.quantize_mx(
+                    out=w1c[:, h * 512 : (h + 1) * 512].bitcast(FP8X4),
+                    scales=w1s[:, h * 512 : (h + 1) * 512],
+                    in_=w1g[:, h * 2048 : (h + 1) * 2048],
+                )
+            b1f = const.tile([P, 4], F32)
+            nc.vector.tensor_copy(out=b1f[:], in_=b1r[:])
+            nc.vector.quantize_mx(out=cb[:, 0:1024].bitcast(FP8X4), scales=sb[:, 0:1024], in_=xg[:, 128:4224])
+            nc.vector.quantize_mx(out=cb[:, 1024:1152].bitcast(FP8X4), scales=sb[:, 1024:1152], in_=xg[:, 4224:4736])
+
+            w2g = pro.tile([P, 2048], BF16, align_bytes=64)
+            w2c = const.tile([P, 512], U32, align_bytes=64)
+            w2s = const.tile([P, 512], U8, align_bytes=64)
+            nc.scalar.copy(
+                out=w2g[:].rearrange("p (n t) -> p n t", t=4),
+                in_=w2r[:].rearrange("p (t n) -> p n t", t=4),
+            )
+            nc.vector.quantize_mx(out=w2c[:].bitcast(FP8X4), scales=w2s[:], in_=w2g[:])
+            b2b = const.tile([P, 512], F32)
+            nc.gpsimd.tensor_copy(out=b2b[:], in_=b2r[:])
+            negm = const.tile([P, 8 * 32], F32)
+            nc.gpsimd.memset(negm[:], 0.0)
+            for m in range(8):
+                for d0 in range(1, 4):
+                    c = 32 * m + d0 * (m + 1)
+                    nc.gpsimd.memset(negm[0 : 32 * d0, c : c + 1], NEG)
+            half = const.tile([P, 4], F32)
+            nc.gpsimd.memset(half[:], 0.5)
+            for m in BLOCKS[1:]:
+                replicate(m)
+        cpool = ctx.enter_context(tc.tile_pool(name="cring", bufs=NC_RING))
 
         quads = []
         for m in BLOCKS:
@@ -153,25 +171,37 @@ def tile_pairconnect_kernel(tc, x, W1, b1, W2, b2, out):
             m = q["m"]
             if "zt" not in q:
                 q["zt"] = {}
-            ci = PADL + 128 * m
+            pieces = []
+            pos = 0
+            while pos < 4:
+                d0, kap = q["tiles"][pos]
+                run = 1
+                while pos + run < 4 and q["tiles"][pos + run][0] == d0:
+                    run += 1
+                while run > 0:
+                    size = 4 if run >= 4 else (2 if run >= 2 else 1)
+                    pieces.append((pos, size, d0, kap))
+                    pos += size
+                    kap += size
+                    run -= size
             for tq in banks:
                 zt = zpool.tile([P, 512], F32, name="zt", tag="z%d" % tq)
                 q["zt"][tq] = zt
-                for pos in range(4):
-                    d0, kap = q["tiles"][pos]
+                for pos, size, d0, kap in pieces:
+                    width = 128 * size
                     cs = PADL + 128 * kap - 32 * d0
                     if d0 % 2 == 0:
                         xjc, xjs = ca, sa
                     else:
                         xjc, xjs = cb, sb
                         cs -= 32
-                    zo = zt[:, 128 * pos : 128 * pos + 128]
+                    zo = zt[:, 128 * pos : 128 * pos + width]
                     nc.tensor.matmul_mx(
                         out=zo,
                         lhsT=w1c[:, tq * 128 : tq * 128 + 128].bitcast(FP8X4),
                         lhsT_scale=w1s[:, tq * 128 : tq * 128 + 128],
-                        rhs=ca[:, ci : ci + 128].bitcast(FP8X4),
-                        rhs_scale=sa[:, ci : ci + 128],
+                        rhs=xic[:, 512 * m : 512 * m + width].bitcast(FP8X4),
+                        rhs_scale=xis[:, 512 * m : 512 * m + width],
                         start=True,
                         stop=False,
                     )
@@ -179,8 +209,8 @@ def tile_pairconnect_kernel(tc, x, W1, b1, W2, b2, out):
                         out=zo,
                         lhsT=w1c[:, 512 + tq * 128 : 512 + tq * 128 + 128].bitcast(FP8X4),
                         lhsT_scale=w1s[:, 512 + tq * 128 : 512 + tq * 128 + 128],
-                        rhs=xjc[:, cs : cs + 128].bitcast(FP8X4),
-                        rhs_scale=xjs[:, cs : cs + 128],
+                        rhs=xjc[:, cs : cs + width].bitcast(FP8X4),
+                        rhs_scale=xjs[:, cs : cs + width],
                         start=False,
                         stop=True,
                     )
@@ -261,11 +291,13 @@ def tile_pairconnect_kernel(tc, x, W1, b1, W2, b2, out):
                     out=junk[:], in_=q["ct"][pos][:], func=ACT.Square, accum_out=st["ssq"][:, col : col + 1]
                 )
                 st["cts"].append(q["ct"][pos])
+            nc.gpsimd.tensor_tensor(
+                out=st["sc"][:, 4 * g : 4 * g + 4], in0=st["ssq"][:, 4 * g : 4 * g + 4], in1=half[:], op=ALU.pow
+            )
 
         def emit_softmax_a(m):
             st = blk[m]
             nd = st["nd"]
-            nc.gpsimd.tensor_tensor(out=st["sc"][:, 0:nd], in0=st["ssq"][:, 0:nd], in1=half[:, 0:nd], op=ALU.pow)
             sk = small.tile([P, 32], F32, name="sk", tag="sk")
             nc.vector.tensor_tensor(out=sk[:, 0:nd], in0=st["sc"][:, 0:nd], in1=negm[:, 32 * m : 32 * m + nd], op=ALU.add)
             mx = small.tile([P, 1], F32, name="mx", tag="mx")
@@ -318,23 +350,25 @@ def tile_pairconnect_kernel(tc, x, W1, b1, W2, b2, out):
                     if st["npe"] == 0:
                         st["ab"] = apool.tile([P, 512], F32, name="ab_acc", tag="ab")
                     dg = dpool.tile([P, P], F32, name="dg", tag="dg")
-                    nc.scalar.activation(out=dg[:], in_=ident[:], func=ACT.Copy, scale=wcol)
+                    nc.gpsimd.tensor_scalar(out=dg[:], in0=ident[:], scalar1=wcol, scalar2=0.0, op0=ALU.mult, op1=ALU.add)
                     st["npe"] += 1
                     nc.tensor.matmul(
                         out=st["ab"][:], lhsT=dg[:], rhs=ct[:], start=(st["npe"] == 1), stop=(st["npe"] == N_PE[m])
                     )
-                elif st["nv"] == 0:
-                    st["o"] = work.tile([P, 512], F32, name="o_acc", tag="o")
-                    nc.vector.tensor_scalar(out=st["o"][:], in0=ct[:], scalar1=wcol, scalar2=None, op0=ALU.mult)
+                elif st["nv"] < 2:
+                    acc = work.tile([P, 512], F32, name="o_acc", tag="o%d" % st["nv"])
+                    st["o%d" % st["nv"]] = acc
+                    nc.vector.tensor_scalar(out=acc[:], in0=ct[:], scalar1=wcol, scalar2=None, op0=ALU.mult)
                     st["nv"] += 1
                 else:
-                    nc.vector.scalar_tensor_tensor(
-                        out=st["o"][:], in0=ct[:], scalar=wcol, in1=st["o"][:], op0=ALU.mult, op1=ALU.add
-                    )
+                    acc = st["o%d" % (st["nv"] % 2)]
+                    nc.vector.scalar_tensor_tensor(out=acc[:], in0=ct[:], scalar=wcol, in1=acc[:], op0=ALU.mult, op1=ALU.add)
                     st["nv"] += 1
                 head["live"] -= 1
                 if st["nv"] + st["npe"] == st["nd"]:
+                    st["o"] = st["o0"]
                     nc.vector.tensor_tensor(out=st["o"][:], in0=st["ab"][:], in1=st["o"][:], op=ALU.add)
+                    nc.vector.tensor_tensor(out=st["o"][:], in0=st["o1"][:], in1=st["o"][:], op=ALU.add)
                     for r in range(4):
                         nc.sync.dma_start(out=out[:, 4 * m + r, :], in_=st["o"][32 * r : 32 * r + 32, :])
 

from contextlib import ExitStack

import concourse.mybir as mybir
from concourse.masks import make_identity

FLOPS = 2 * 1024 * 1024 * 512 + 2 * 16896 * 512 * 512

F32 = mybir.dt.float32
BF16 = mybir.dt.bfloat16
U32 = mybir.dt.uint32
U8 = mybir.dt.uint8
I32 = mybir.dt.int32
FP8X4 = mybir.dt.float8_e4m3fn_x4
ALU = mybir.AluOpType
ACT = mybir.ActivationFunctionType
AX = mybir.AxisListType

P = 128
PADL = 128
NCOL = PADL + 1024 + 32
NEG = -1.0e9
NC_RING = 52
N_PE = (2, 3, 5, 6, 8, 10, 11, 13)
BLOCKS = (7, 6, 5, 4, 3, 2, 1, 0)
LAG = 2
RATE = 6


def regroup_on_scalar(k):
    return False


def tile_pairconnect_kernel(tc, x, W1, b1, W2, b2, out):
    nc = tc.nc
    with ExitStack() as ctx:
        const = ctx.enter_context(tc.tile_pool(name="const", bufs=1))
        work = ctx.enter_context(tc.tile_pool(name="work", bufs=3))
        small = ctx.enter_context(tc.tile_pool(name="small", bufs=5))
        dpool = ctx.enter_context(tc.tile_pool(name="diag", bufs=4))
        zpool = ctx.enter_context(tc.psum_pool(name="zps", bufs=1))
        ppool = ctx.enter_context(tc.psum_pool(name="pps", bufs=3))
        apool = ctx.enter_context(tc.psum_pool(name="aps", bufs=1))

        with tc.tile_pool(name="pro", bufs=1) as pro:
            xr = pro.tile([P, 4096], BF16)
            xv = x.flatten_outer_dims().rearrange("(n p) k -> p n k", p=P)
            xrv = xr[:].rearrange("p (n k) -> p n k", n=8)
            nc.sync.dma_start(out=xrv[:, 0:4, :], in_=xv[:, 0:4, :])
            nc.sync.dma_start(out=xrv[:, 4:8, :], in_=xv[:, 4:8, :])
            w1r = pro.tile([P, 4096], BF16)
            nc.sync.dma_start(
                out=w1r[:].rearrange("p (a f) -> p a f", a=4),
                in_=W1.rearrange("(a q e) c -> q a (e c)", a=4, q=P, e=2),
            )
            w2r = pro.tile([P, 2048], BF16)
            nc.sync.dma_start(
                out=w2r[:].rearrange("p (t n) -> p t n", t=4),
                in_=W2.rearrange("(p t) n -> p t n", t=4),
            )
            b1r = pro.tile([P, 4], BF16)
            nc.sync.dma_start(out=b1r[:], in_=b1.rearrange("(p t) -> p t", t=4))
            b2r = pro.tile([P, 512], BF16)
            nc.sync.dma_start(out=b2r[:], in_=b2.partition_broadcast(P))

            ident = const.tile([P, P], F32)
            make_identity(nc, ident[:])

            xg = pro.tile([P, NCOL * 4], BF16, align_bytes=64)
            xg32 = xg[:].bitcast(F32)
            nc.vector.memset(xg32[:, 0 : 2 * PADL], 0.0)
            nc.vector.memset(xg32[:, 2 * (PADL + 1024) : 2 * NCOL], 0.0)
            xr32 = xr[:].bitcast(F32)
            xbody = xg32[:, 2 * PADL : 2 * PADL + 2048].rearrange(
                "p (i b u) -> p i b u", i=32, b=32, u=2
            )
            for j in range(4):
                pt = ppool.tile([P, 512], F32, tag="pp")
                for u in range(2):
                    for n2 in range(2):
                        off = u * 256 + n2 * 128
                        src0 = (2 * j + n2) * 256 + u * 128
                        nc.tensor.transpose(pt[:, off : off + 128], xr32[:, src0 : src0 + 128], ident[:])
                src = pt[:].rearrange("p (u c i) -> p i c u", u=2, c=8, i=32)
                dst = xbody[:, :, 8 * j : 8 * j + 8, :]
                if j % 2 == 0:
                    nc.vector.tensor_copy(out=dst, in_=src)
                else:
                    nc.scalar.copy(out=dst, in_=src)

            ca = const.tile([P, 1152], U32, align_bytes=64)
            sa = const.tile([P, 1152], U8, align_bytes=64)
            cb = const.tile([P, 1152], U32, align_bytes=64)
            sb = const.tile([P, 1152], U8, align_bytes=64)

            w1g = pro.tile([P, 4096], BF16, align_bytes=64)
            w1c = const.tile([P, 1024], U32, align_bytes=64)
            w1s = const.tile([P, 1024], U8, align_bytes=64)
            for h in range(2):
                dst = w1g[:, h * 2048 : (h + 1) * 2048].rearrange("p (q m t) -> p q m t", q=4, m=P, t=4)
                src = w1r[:, h * 2048 : (h + 1) * 2048].rearrange("p (t m q) -> p q m t", t=4, m=P, q=4)
                if h == 0:
                    nc.vector.tensor_copy(out=dst, in_=src)
                else:
                    nc.scalar.copy(out=dst, in_=src)
            nc.vector.quantize_mx(out=ca[:, 0:1024].bitcast(FP8X4), scales=sa[:, 0:1024], in_=xg[:, 0:4096])
            nc.vector.quantize_mx(out=ca[:, 1024:1152].bitcast(FP8X4), scales=sa[:, 1024:1152], in_=xg[:, 4096:4608])
            xic = const.tile([P, 8 * 512], U32, align_bytes=64)
            xis = const.tile([P, 8 * 512], U8, align_bytes=64)

            def replicate(m):
                ci = PADL + 128 * m
                nc.vector.tensor_copy(
                    out=xic[:, 512 * m : 512 * m + 512].bitcast(I32).rearrange("p (r w) -> p r w", r=4),
                    in_=ca[:, ci : ci + 128].bitcast(I32).unsqueeze(1).to_broadcast([P, 4, 128]),
                )
                nc.vector.tensor_copy(
                    out=xis[:, 512 * m : 512 * m + 512].bitcast(I32).rearrange("p (r w) -> p r w", r=4),
                    in_=sa[:, ci : ci + 128].bitcast(I32).unsqueeze(1).to_broadcast([P, 4, 32]),
                )

            replicate(BLOCKS[0])
            for h in range(2):
                nc.vector.quantize_mx(
                    out=w1c[:, h * 512 : (h + 1) * 512].bitcast(FP8X4),
                    scales=w1s[:, h * 512 : (h + 1) * 512],
                    in_=w1g[:, h * 2048 : (h + 1) * 2048],
                )
            b1f = const.tile([P, 4], F32)
            nc.vector.tensor_copy(out=b1f[:], in_=b1r[:])
            nc.vector.quantize_mx(out=cb[:, 0:1024].bitcast(FP8X4), scales=sb[:, 0:1024], in_=xg[:, 128:4224])
            nc.vector.quantize_mx(out=cb[:, 1024:1152].bitcast(FP8X4), scales=sb[:, 1024:1152], in_=xg[:, 4224:4736])

            w2g = pro.tile([P, 2048], BF16, align_bytes=64)
            w2c = const.tile([P, 512], U32, align_bytes=64)
            w2s = const.tile([P, 512], U8, align_bytes=64)
            nc.scalar.copy(
                out=w2g[:].rearrange("p (n t) -> p n t", t=4),
                in_=w2r[:].rearrange("p (t n) -> p n t", t=4),
            )
            nc.vector.quantize_mx(out=w2c[:].bitcast(FP8X4), scales=w2s[:], in_=w2g[:])
            b2b = const.tile([P, 512], F32)
            nc.gpsimd.tensor_copy(out=b2b[:], in_=b2r[:])
            negm = const.tile([P, 8 * 32], F32)
            nc.gpsimd.memset(negm[:], 0.0)
            for m in range(8):
                for d0 in range(1, 4):
                    c = 32 * m + d0 * (m + 1)
                    nc.gpsimd.memset(negm[0 : 32 * d0, c : c + 1], NEG)
            half = const.tile([P, 4], F32)
            nc.gpsimd.memset(half[:], 0.5)
            for m in BLOCKS[1:]:
                replicate(m)
        cpool = ctx.enter_context(tc.tile_pool(name="cring", bufs=NC_RING))

        quads = []
        for m in BLOCKS:
            tiles = [(d0, kap) for d0 in range(4) for kap in range(m + 1)]
            for g in range(m + 1):
                quads.append({"m": m, "g": g, "tiles": tiles[4 * g : 4 * g + 4], "last": g == m})
        nq = len(quads)
        blk = {}
        for m in BLOCKS:
            blk[m] = {"m": m, "nd": 4 * (m + 1), "cts": [], "nv": 0, "npe": 0, "fin": False}
        pend = []
        head = {"w": 0, "live": 0, "k": 0}

        def emit_z(k, banks):
            if k >= nq:
                return
            q = quads[k]
            m = q["m"]
            if "zt" not in q:
                q["zt"] = {}
            pieces = []
            pos = 0
            while pos < 4:
                d0, kap = q["tiles"][pos]
                run = 1
                while pos + run < 4 and q["tiles"][pos + run][0] == d0:
                    run += 1
                while run > 0:
                    size = 4 if run >= 4 else (2 if run >= 2 else 1)
                    pieces.append((pos, size, d0, kap))
                    pos += size
                    kap += size
                    run -= size
            for tq in banks:
                zt = zpool.tile([P, 512], F32, name="zt", tag="z%d" % tq)
                q["zt"][tq] = zt
                for pos, size, d0, kap in pieces:
                    width = 128 * size
                    cs = PADL + 128 * kap - 32 * d0
                    if d0 % 2 == 0:
                        xjc, xjs = ca, sa
                    else:
                        xjc, xjs = cb, sb
                        cs -= 32
                    zo = zt[:, 128 * pos : 128 * pos + width]
                    nc.tensor.matmul_mx(
                        out=zo,
                        lhsT=w1c[:, tq * 128 : tq * 128 + 128].bitcast(FP8X4),
                        lhsT_scale=w1s[:, tq * 128 : tq * 128 + 128],
                        rhs=xic[:, 512 * m : 512 * m + width].bitcast(FP8X4),
                        rhs_scale=xis[:, 512 * m : 512 * m + width],
                        start=True,
                        stop=False,
                    )
                    nc.tensor.matmul_mx(
                        out=zo,
                        lhsT=w1c[:, 512 + tq * 128 : 512 + tq * 128 + 128].bitcast(FP8X4),
                        lhsT_scale=w1s[:, 512 + tq * 128 : 512 + tq * 128 + 128],
                        rhs=xjc[:, cs : cs + width].bitcast(FP8X4),
                        rhs_scale=xjs[:, cs : cs + width],
                        start=False,
                        stop=True,
                    )

        def emit_regroup(k, engine):
            q = quads[k]
            hg = work.tile([P, 2048], BF16, name="hg", tag="hg", align_bytes=64)
            q["hg"] = hg
            dst = hg[:].rearrange("p (c i t) -> p c t i", i=4, t=4)
            src = q["hp"][:].rearrange("p (t c i) -> p c t i", t=4, i=4)
            if engine == "S":
                nc.scalar.copy(out=dst, in_=src)
            else:
                nc.vector.tensor_copy(out=dst, in_=src)

        def emit_gelu(k):
            if k >= nq:
                return
            q = quads[k]
            hp = work.tile([P, 2048], BF16, name="hp", tag="hp")
            q["hp"] = hp
            for tq in range(4):
                nc.scalar.activation(
                    out=hp[:, tq * 512 : (tq + 1) * 512],
                    in_=q["zt"][tq][:],
                    func=ACT.Gelu,
                    bias=b1f[:, tq : tq + 1],
                    scale=1.0,
                )
            if regroup_on_scalar(k):
                emit_regroup(k, "S")

        def emit_quant(k):
            q = quads[k]
            if not regroup_on_scalar(k):
                emit_regroup(k, "V")
            hc = work.tile([P, 512], U32, name="hc", tag="hc", align_bytes=64)
            hs = work.tile([P, 512], U8, name="hs", tag="hs", align_bytes=64)
            q["hc"] = hc
            q["hs"] = hs
            q["pp"] = {}
            q["ct"] = {}
            nc.vector.quantize_mx(out=hc[:].bitcast(FP8X4), scales=hs[:], in_=q["hg"][:])

        def emit_s2(k, pos):
            q = quads[k]
            pp = ppool.tile([P, 512], F32, name="pp", tag="pp")
            q["pp"][pos] = pp
            nc.tensor.matmul_mx(
                out=pp[:],
                lhsT=q["hc"][:, 128 * pos : 128 * pos + 128].bitcast(FP8X4),
                lhsT_scale=q["hs"][:, 128 * pos : 128 * pos + 128],
                rhs=w2c[:].bitcast(FP8X4),
                rhs_scale=w2s[:],
                start=True,
                stop=True,
            )

        def emit_evac(k, pos):
            q = quads[k]
            ct = cpool.tile([P, 512], F32, name="ct", tag="c")
            head["live"] += 1
            assert head["live"] <= NC_RING
            q["ct"][pos] = ct
            nc.vector.tensor_tensor(out=ct[:], in0=q["pp"][pos][:], in1=b2b[:], op=ALU.add)

        def emit_square(k):
            q = quads[k]
            st = blk[q["m"]]
            g = q["g"]
            if g == 0:
                st["ssq"] = small.tile([P, 32], F32, name="ssq", tag="ssq")
                st["sc"] = small.tile([P, 32], F32, name="sc", tag="sc")
            for pos in range(4):
                col = 4 * g + pos
                junk = work.tile([P, 512], BF16, name="junk", tag="junk")
                nc.scalar.activation(
                    out=junk[:], in_=q["ct"][pos][:], func=ACT.Square, accum_out=st["ssq"][:, col : col + 1]
                )
                st["cts"].append(q["ct"][pos])
            nc.gpsimd.tensor_tensor(
                out=st["sc"][:, 4 * g : 4 * g + 4], in0=st["ssq"][:, 4 * g : 4 * g + 4], in1=half[:], op=ALU.pow
            )

        def emit_softmax_a(m):
            st = blk[m]
            nd = st["nd"]
            sk = small.tile([P, 32], F32, name="sk", tag="sk")
            nc.vector.tensor_tensor(out=sk[:, 0:nd], in0=st["sc"][:, 0:nd], in1=negm[:, 32 * m : 32 * m + nd], op=ALU.add)
            mx = small.tile([P, 1], F32, name="mx", tag="mx")
            nc.vector.tensor_reduce(out=mx[:], in_=sk[:, 0:nd], axis=AX.X, op=ALU.max)
            nh = small.tile([P, 1], F32, name="nh", tag="nh")
            nc.vector.tensor_scalar(out=nh[:], in0=mx[:], scalar1=-0.5, scalar2=None, op0=ALU.mult)
            st["sk"] = sk
            st["nh"] = nh

        def emit_tanh(m):
            st = blk[m]
            nd = st["nd"]
            th = small.tile([P, 32], F32, name="th", tag="th")
            nc.scalar.activation(out=th[:, 0:nd], in_=st["sk"][:, 0:nd], func=ACT.Tanh, bias=st["nh"][:, 0:1], scale=0.5)
            st["th"] = th

        def emit_softmax_b(m):
            st = blk[m]
            nd = st["nd"]
            th = st["th"]
            bq = small.tile([P, 32], F32, name="bq", tag="bq")
            nc.vector.tensor_scalar(out=bq[:, 0:nd], in0=th[:, 0:nd], scalar1=-1.0, scalar2=1.0, op0=ALU.mult, op1=ALU.add)
            rb = small.tile([P, 32], F32, name="rb", tag="rb")
            nc.vector.reciprocal(out=rb[:, 0:nd], in_=bq[:, 0:nd])
            ex = small.tile([P, 32], F32, name="ex", tag="ex")
            se = small.tile([P, 1], F32, name="se", tag="se")
            nc.vector.scalar_tensor_tensor(
                out=ex[:, 0:nd], in0=th[:, 0:nd], scalar=1.0, in1=rb[:, 0:nd], op0=ALU.add, op1=ALU.mult, accum_out=se[:]
            )
            rs = small.tile([P, 1], F32, name="rs", tag="rs")
            nc.vector.reciprocal(out=rs[:], in_=se[:])
            wt = small.tile([P, 32], F32, name="wt", tag="wt")
            nc.vector.tensor_scalar(out=wt[:, 0:nd], in0=ex[:, 0:nd], scalar1=rs[:, 0:1], scalar2=None, op0=ALU.mult)
            st["wt"] = wt
            npe = N_PE[m]
            for col in range(nd):
                on_pe = ((col + 1) * npe) // nd > (col * npe) // nd
                pend.append((m, col, on_pe, head["k"]))

        def emit_wacc(count, k_now):
            for unused in range(count):
                if head["w"] >= len(pend) or pend[head["w"]][3] + LAG > k_now:
                    return
                m, col, on_pe, unused_k = pend[head["w"]]
                head["w"] += 1
                st = blk[m]
                wcol = st["wt"][:, col : col + 1]
                ct = st["cts"][col]
                if on_pe:
                    if st["npe"] == 0:
                        st["ab"] = apool.tile([P, 512], F32, name="ab_acc", tag="ab")
                    dg = dpool.tile([P, P], F32, name="dg", tag="dg")
                    nc.gpsimd.tensor_scalar(out=dg[:], in0=ident[:], scalar1=wcol, scalar2=0.0, op0=ALU.mult, op1=ALU.add)
                    st["npe"] += 1
                    nc.tensor.matmul(
                        out=st["ab"][:], lhsT=dg[:], rhs=ct[:], start=(st["npe"] == 1), stop=(st["npe"] == N_PE[m])
                    )
                elif st["nv"] < 2:
                    acc = work.tile([P, 512], F32, name="o_acc", tag="o%d" % st["nv"])
                    st["o%d" % st["nv"]] = acc
                    nc.vector.tensor_scalar(out=acc[:], in0=ct[:], scalar1=wcol, scalar2=None, op0=ALU.mult)
                    st["nv"] += 1
                else:
                    acc = st["o%d" % (st["nv"] % 2)]
                    nc.vector.scalar_tensor_tensor(out=acc[:], in0=ct[:], scalar=wcol, in1=acc[:], op0=ALU.mult, op1=ALU.add)
                    st["nv"] += 1
                head["live"] -= 1
                if st["nv"] + st["npe"] == st["nd"]:
                    st["o"] = st["o0"]
                    nc.vector.tensor_tensor(out=st["o"][:], in0=st["ab"][:], in1=st["o"][:], op=ALU.add)
                    nc.vector.tensor_tensor(out=st["o"][:], in0=st["o1"][:], in1=st["o"][:], op=ALU.add)
                    for r in range(4):
                        nc.sync.dma_start(out=out[:, 4 * m + r, :], in_=st["o"][32 * r : 32 * r + 32, :])

        for k in range(nq):
            head["k"] = k
            emit_z(k, (0, 1, 2, 3))
            emit_gelu(k)
            emit_quant(k)
            for pos in range(4):
                emit_s2(k, pos)
                emit_evac(k, pos)
            emit_square(k)
            if quads[k]["last"]:
                emit_softmax_a(quads[k]["m"])
                emit_tanh(quads[k]["m"])
                emit_softmax_b(quads[k]["m"])
            emit_wacc(RATE, k)
        emit_wacc(1000, nq + LAG)
        assert head["w"] == 144
